import numpy as np
import ml_dtypes

BF16 = ml_dtypes.bfloat16


def bf(x):
    return np.asarray(x, np.float32).astype(BF16)


def f32(x):
    return np.asarray(x, np.float32)


def f64(x):
    return np.asarray(x).astype(np.float64)


def striped(idx):
    return np.tile(idx.reshape(-1, 16).T, (8, 1))


C, S, K, N, T = 256, 4096, 2, 2048, 1000
MASS = 0.3829249225480262


def setup_inputs():
    return {"fc": f32(np.random.standard_normal((K, C, S))), "fc_all": f32(np.random.standard_normal((C, T))), "w_sel": f32(0.1 * np.random.standard_normal((1, N))), "w_all": f32(0.1 * np.random.standard_normal((1, T))), "b": f32(1.0 + 0.1 * np.random.standard_normal((1,))), "offs": striped(np.random.permutation(S)[:N])}


def reference(fc, fc_all, w_sel, w_all, b, offs):
    idx = offs[:16].T.reshape(-1)
    piece = N // K
    acc = (f64(fc_all) * MASS * f64(w_all)).sum(axis=1, keepdims=True)
    for k in range(K):
        sl = slice(k * piece, (k + 1) * piece)
        acc = acc + (f64(fc)[k][:, idx[sl]] * MASS * f64(w_sel)[:, sl]).sum(axis=1, keepdims=True)
    return acc + f64(b)[0]

@@ -1,0 +1,72 @@
+import concourse.masks as masks
+import concourse.mybir as mybir
+
+F32 = mybir.dt.float32
+U16 = mybir.dt.uint16
+MULT = mybir.AluOpType.mult
+IDENTITY = mybir.ActivationFunctionType.Identity
+
+P = 128
+LAYERS = 2
+SAMPLES = 256
+UNITS = 4096
+PICKED = 1024
+WHOLE = 1000
+BLOCKS = SAMPLES // P
+MASS = 0.3829249225480262
+
+FLOPS = 2 * SAMPLES * (LAYERS * PICKED + WHOLE)
+
+
+def tile_average_model_fwrf_kernel(tc, fc, fc_all, w_sel, w_all, b, offs, out):
+    nc = tc.nc
+    with (
+        tc.tile_pool(name="held", bufs=1) as held,
+        tc.tile_pool(name="work", bufs=2) as work,
+        tc.psum_pool(name="psum", bufs=1) as psum,
+    ):
+        offsets = held.tile([P, LAYERS * PICKED // 16], U16, name="offsets")
+        nc.sync.dma_start(offsets[:], offs)
+
+        w_sel_rows = held.tile([P, LAYERS * PICKED], F32, name="w_sel_rows")
+        nc.sync.dma_start(w_sel_rows[:], w_sel.rearrange("one n -> (one n)").partition_broadcast(P))
+        w_all_rows = held.tile([P, WHOLE], F32, name="w_all_rows")
+        nc.scalar.dma_start(w_all_rows[:], w_all.rearrange("one n -> (one n)").partition_broadcast(P))
+        bias = held.tile([BLOCKS, 1], F32, name="bias")
+        nc.scalar.dma_start(bias[:], b.partition_broadcast(BLOCKS))
+
+        identity = held.tile([P, P], F32, name="identity")
+        masks.make_identity(nc, identity[:])
+
+        all_sums = held.tile([P, BLOCKS], F32, name="all_sums")
+        sel_sums = held.tile([P, LAYERS * BLOCKS], F32, name="sel_sums")
+
+        for blk in range(BLOCKS):
+            kept = held.tile([P, WHOLE], F32, name=f"kept{blk}")
+            nc.scalar.dma_start(kept[:], fc_all[blk * P : (blk + 1) * P, :])
+            kept_prod = work.tile([P, WHOLE], F32, name="kept_prod")
+            nc.vector.scalar_tensor_tensor(
+                kept_prod[:], kept[:], 1.0, w_all_rows[:], MULT, MULT,
+                accum_out=all_sums[:, blk : blk + 1],
+            )
+
+        for layer in range(LAYERS):
+            for blk in range(BLOCKS):
+                window = held.tile([P, UNITS], F32, name=f"window{layer}{blk}")
+                nc.sync.dma_start(window[:], fc[layer, blk * P : (blk + 1) * P, :])
+                picked = window[:].indirect(offsets[:, layer * (PICKED // 16) : (layer + 1) * (PICKED // 16)])
+                prod = work.tile([P, PICKED], F32, name="prod")
+                nc.vector.tensor_tensor(prod[:], picked, w_sel_rows[:, layer * PICKED : (layer + 1) * PICKED], MULT)
+                col = layer * BLOCKS + blk
+                nc.scalar.activation(prod[:], prod[:], IDENTITY, accum_out=sel_sums[:, col : col + 1])
+
+        total = psum.tile([BLOCKS, P], F32, name="total")
+        nc.tensor.matmul(total[:], all_sums[:], identity[:], start=True, stop=False)
+        for layer in range(LAYERS):
+            nc.tensor.matmul(
+                total[:], sel_sums[:, layer * BLOCKS : (layer + 1) * BLOCKS], identity[:],
+                start=False, stop=(layer == LAYERS - 1),
+            )
+        result = held.tile([BLOCKS, P], F32, name="result")
+        nc.scalar.activation(result[:], total[:], IDENTITY, bias=bias[:], scale=MASS)
+        nc.sync.dma_start(out.rearrange("(blk c) one -> blk (c one)", blk=BLOCKS), result[:])

@@ -13,6 +13,7 @@ UNITS = 4096
 PICKED = 1024
 WHOLE = 1000
 BLOCKS = SAMPLES // P
+BANK = 512
 MASS = 0.3829249225480262
 
 FLOPS = 2 * SAMPLES * (LAYERS * PICKED + WHOLE)
@@ -23,50 +24,71 @@ def tile_average_model_fwrf_kernel(tc, fc, fc_all, w_sel, w_all, b, offs, out):
     with (
         tc.tile_pool(name="held", bufs=1) as held,
         tc.tile_pool(name="work", bufs=2) as work,
+        tc.psum_pool(name="banks", bufs=2) as banks,
         tc.psum_pool(name="psum", bufs=1) as psum,
     ):
         offsets = held.tile([P, LAYERS * PICKED // 16], U16, name="offsets")
         nc.sync.dma_start(offsets[:], offs)
 
-        w_sel_rows = held.tile([P, LAYERS * PICKED], F32, name="w_sel_rows")
-        nc.sync.dma_start(w_sel_rows[:], w_sel.rearrange("one n -> (one n)").partition_broadcast(P))
-        w_all_rows = held.tile([P, WHOLE], F32, name="w_all_rows")
-        nc.scalar.dma_start(w_all_rows[:], w_all.rearrange("one n -> (one n)").partition_broadcast(P))
+        w_sel_row = held.tile([1, LAYERS * PICKED], F32, name="w_sel_row")
+        nc.sync.dma_start(w_sel_row[:], w_sel)
+        w_all_row = held.tile([1, WHOLE], F32, name="w_all_row")
+        nc.sync.dma_start(w_all_row[:], w_all)
         bias = held.tile([BLOCKS, 1], F32, name="bias")
-        nc.scalar.dma_start(bias[:], b.partition_broadcast(BLOCKS))
+        nc.sync.dma_start(bias[:], b.partition_broadcast(BLOCKS))
+
+        windows = {}
+        for layer in range(LAYERS):
+            for blk in range(BLOCKS):
+                windows[layer, blk] = held.tile([P, UNITS], F32, name=f"window{layer}{blk}")
+                nc.sync.dma_start(windows[layer, blk][:], fc[layer, blk * P : (blk + 1) * P, :])
+        kept = {}
+        for blk in range(BLOCKS):
+            kept[blk] = held.tile([P, WHOLE], F32, name=f"kept{blk}")
+            nc.sync.dma_start(kept[blk][:], fc_all[blk * P : (blk + 1) * P, :])
 
         identity = held.tile([P, P], F32, name="identity")
         masks.make_identity(nc, identity[:])
+        ones = held.tile([1, P], F32, name="ones")
+        nc.gpsimd.memset(ones[:], 1.0)
 
-        all_sums = held.tile([P, BLOCKS], F32, name="all_sums")
+        w_sel_rows = held.tile([P, LAYERS * PICKED], F32, name="w_sel_rows")
+        w_all_rows = held.tile([P, WHOLE], F32, name="w_all_rows")
+        for row, rows in ((w_sel_row, w_sel_rows), (w_all_row, w_all_rows)):
+            width = rows.shape[1]
+            for start in range(0, width, BANK):
+                end = min(start + BANK, width)
+                bank = banks.tile([P, BANK], F32, name="bank")
+                nc.tensor.matmul(bank[:, : end - start], ones[:], row[:, start:end], start=True, stop=True)
+                nc.scalar.copy(rows[:, start:end], bank[:, : end - start])
+
         sel_sums = held.tile([P, LAYERS * BLOCKS], F32, name="sel_sums")
-
-        for blk in range(BLOCKS):
-            kept = held.tile([P, WHOLE], F32, name=f"kept{blk}")
-            nc.scalar.dma_start(kept[:], fc_all[blk * P : (blk + 1) * P, :])
-            kept_prod = work.tile([P, WHOLE], F32, name="kept_prod")
-            nc.vector.scalar_tensor_tensor(
-                kept_prod[:], kept[:], 1.0, w_all_rows[:], MULT, MULT,
-                accum_out=all_sums[:, blk : blk + 1],
-            )
+        all_sums = held.tile([P, BLOCKS], F32, name="all_sums")
 
         for layer in range(LAYERS):
             for blk in range(BLOCKS):
-                window = held.tile([P, UNITS], F32, name=f"window{layer}{blk}")
-                nc.sync.dma_start(window[:], fc[layer, blk * P : (blk + 1) * P, :])
-                picked = window[:].indirect(offsets[:, layer * (PICKED // 16) : (layer + 1) * (PICKED // 16)])
+                picked = windows[layer, blk][:].indirect(
+                    offsets[:, layer * (PICKED // 16) : (layer + 1) * (PICKED // 16)]
+                )
                 prod = work.tile([P, PICKED], F32, name="prod")
                 nc.vector.tensor_tensor(prod[:], picked, w_sel_rows[:, layer * PICKED : (layer + 1) * PICKED], MULT)
                 col = layer * BLOCKS + blk
                 nc.scalar.activation(prod[:], prod[:], IDENTITY, accum_out=sel_sums[:, col : col + 1])
 
+        for blk in range(BLOCKS):
+            kept_prod = work.tile([P, WHOLE], F32, name="kept_prod")
+            nc.vector.scalar_tensor_tensor(
+                kept_prod[:], kept[blk][:], 1.0, w_all_rows[:], MULT, MULT,
+                accum_out=all_sums[:, blk : blk + 1],
+            )
+
         total = psum.tile([BLOCKS, P], F32, name="total")
-        nc.tensor.matmul(total[:], all_sums[:], identity[:], start=True, stop=False)
         for layer in range(LAYERS):
             nc.tensor.matmul(
                 total[:], sel_sums[:, layer * BLOCKS : (layer + 1) * BLOCKS], identity[:],
-                start=False, stop=(layer == LAYERS - 1),
+                start=(layer == 0), stop=False,
             )
+        nc.tensor.matmul(total[:], all_sums[:], identity[:], start=False, stop=True)
         result = held.tile([BLOCKS, P], F32, name="result")
         nc.scalar.activation(result[:], total[:], IDENTITY, bias=bias[:], scale=MASS)
         nc.sync.dma_start(out.rearrange("(blk c) one -> blk (c one)", blk=BLOCKS), result[:])

@@ -1,9 +1,9 @@
-import concourse.masks as masks
 import concourse.mybir as mybir
 
 F32 = mybir.dt.float32
 U16 = mybir.dt.uint16
 MULT = mybir.AluOpType.mult
+ADD = mybir.AluOpType.add
 IDENTITY = mybir.ActivationFunctionType.Identity
 
 P = 128
@@ -14,6 +14,7 @@ PICKED = 1024
 WHOLE = 1000
 BLOCKS = SAMPLES // P
 BANK = 512
+SQUARE = 32
 MASS = 0.3829249225480262
 
 FLOPS = 2 * SAMPLES * (LAYERS * PICKED + WHOLE)
@@ -25,7 +26,6 @@ def tile_average_model_fwrf_kernel(tc, fc, fc_all, w_sel, w_all, b, offs, out):
         tc.tile_pool(name="held", bufs=1) as held,
         tc.tile_pool(name="work", bufs=2) as work,
         tc.psum_pool(name="banks", bufs=2) as banks,
-        tc.psum_pool(name="psum", bufs=1) as psum,
     ):
         offsets = held.tile([P, LAYERS * PICKED // 16], U16, name="offsets")
         nc.sync.dma_start(offsets[:], offs)
@@ -34,8 +34,8 @@ def tile_average_model_fwrf_kernel(tc, fc, fc_all, w_sel, w_all, b, offs, out):
         nc.sync.dma_start(w_sel_row[:], w_sel)
         w_all_row = held.tile([1, WHOLE], F32, name="w_all_row")
         nc.sync.dma_start(w_all_row[:], w_all)
-        bias = held.tile([BLOCKS, 1], F32, name="bias")
-        nc.sync.dma_start(bias[:], b.partition_broadcast(BLOCKS))
+        b_row = held.tile([1, 1], F32, name="b_row")
+        nc.sync.dma_start(b_row[:], b.unsqueeze(0))
 
         windows = {}
         for layer in range(LAYERS):
@@ -47,14 +47,13 @@ def tile_average_model_fwrf_kernel(tc, fc, fc_all, w_sel, w_all, b, offs, out):
             kept[blk] = held.tile([P, WHOLE], F32, name=f"kept{blk}")
             nc.sync.dma_start(kept[blk][:], fc_all[blk * P : (blk + 1) * P, :])
 
-        identity = held.tile([P, P], F32, name="identity")
-        masks.make_identity(nc, identity[:])
         ones = held.tile([1, P], F32, name="ones")
         nc.gpsimd.memset(ones[:], 1.0)
 
         w_sel_rows = held.tile([P, LAYERS * PICKED], F32, name="w_sel_rows")
         w_all_rows = held.tile([P, WHOLE], F32, name="w_all_rows")
-        for row, rows in ((w_sel_row, w_sel_rows), (w_all_row, w_all_rows)):
+        b_rows = held.tile([P, 1], F32, name="b_rows")
+        for row, rows in ((w_sel_row, w_sel_rows), (w_all_row, w_all_rows), (b_row, b_rows)):
             width = rows.shape[1]
             for start in range(0, width, BANK):
                 end = min(start + BANK, width)
@@ -62,7 +61,8 @@ def tile_average_model_fwrf_kernel(tc, fc, fc_all, w_sel, w_all, b, offs, out):
                 nc.tensor.matmul(bank[:, : end - start], ones[:], row[:, start:end], start=True, stop=True)
                 nc.scalar.copy(rows[:, start:end], bank[:, : end - start])
 
-        sel_sums = held.tile([P, LAYERS * BLOCKS], F32, name="sel_sums")
+        sel_sums = held.tile([P, BLOCKS * LAYERS], F32, name="sel_sums")
+        sel_total = held.tile([P, BLOCKS], F32, name="sel_total")
         all_sums = held.tile([P, BLOCKS], F32, name="all_sums")
 
         for layer in range(LAYERS):
@@ -72,23 +72,31 @@ def tile_average_model_fwrf_kernel(tc, fc, fc_all, w_sel, w_all, b, offs, out):
                 )
                 prod = work.tile([P, PICKED], F32, name="prod")
                 nc.vector.tensor_tensor(prod[:], picked, w_sel_rows[:, layer * PICKED : (layer + 1) * PICKED], MULT)
-                col = layer * BLOCKS + blk
-                nc.scalar.activation(prod[:], prod[:], IDENTITY, accum_out=sel_sums[:, col : col + 1])
+                col = blk * LAYERS + layer
+                nc.scalar.activation(prod[:], prod[:], IDENTITY, scale=MASS, accum_out=sel_sums[:, col : col + 1])
+
+        for blk in range(BLOCKS):
+            both = work.tile([P, LAYERS], F32, name="both")
+            nc.scalar.activation(
+                both[:], sel_sums[:, blk * LAYERS : (blk + 1) * LAYERS], IDENTITY,
+                accum_out=sel_total[:, blk : blk + 1],
+            )
 
         for blk in range(BLOCKS):
             kept_prod = work.tile([P, WHOLE], F32, name="kept_prod")
             nc.vector.scalar_tensor_tensor(
-                kept_prod[:], kept[blk][:], 1.0, w_all_rows[:], MULT, MULT,
+                kept_prod[:], kept[blk][:], MASS, w_all_rows[:], MULT, MULT,
                 accum_out=all_sums[:, blk : blk + 1],
             )
 
-        total = psum.tile([BLOCKS, P], F32, name="total")
-        for layer in range(LAYERS):
-            nc.tensor.matmul(
-                total[:], sel_sums[:, layer * BLOCKS : (layer + 1) * BLOCKS], identity[:],
-                start=(layer == 0), stop=False,
+        columns = held.tile([P, SQUARE], F32, name="columns", align_bytes=64)
+        nc.gpsimd.memset(columns[:], 0.0)
+        nc.vector.scalar_tensor_tensor(columns[:, 0:BLOCKS], all_sums[:], b_rows[:], sel_total[:], ADD, ADD)
+
+        squares = held.tile([P, SQUARE], F32, name="squares", align_bytes=64)
+        nc.vector.transpose(squares[:], columns[:])
+        for blk in range(BLOCKS):
+            nc.sync.dma_start(
+                out[blk * P : (blk + 1) * P, :].rearrange("(q i) one -> q (i one)", i=SQUARE),
+                squares[blk:P:SQUARE, :],
             )
-        nc.tensor.matmul(total[:], all_sums[:], identity[:], start=False, stop=True)
-        result = held.tile([BLOCKS, P], F32, name="result")
-        nc.scalar.activation(result[:], total[:], IDENTITY, bias=bias[:], scale=MASS)
-        nc.sync.dma_start(out.rearrange("(blk c) one -> blk (c one)", blk=BLOCKS), result[:])

@@ -31,11 +31,11 @@ def tile_average_model_fwrf_kernel(tc, fc, fc_all, w_sel, w_all, b, offs, out):
         nc.sync.dma_start(offsets[:], offs)
 
         w_sel_row = held.tile([1, LAYERS * PICKED], F32, name="w_sel_row")
-        nc.sync.dma_start(w_sel_row[:], w_sel)
+        nc.scalar.dma_start(w_sel_row[:], w_sel)
         w_all_row = held.tile([1, WHOLE], F32, name="w_all_row")
-        nc.sync.dma_start(w_all_row[:], w_all)
+        nc.scalar.dma_start(w_all_row[:], w_all)
         b_row = held.tile([1, 1], F32, name="b_row")
-        nc.sync.dma_start(b_row[:], b.unsqueeze(0))
+        nc.scalar.dma_start(b_row[:], b.unsqueeze(0))
 
         windows = {}
         for layer in range(LAYERS):

@@ -27,21 +27,21 @@ def tile_average_model_fwrf_kernel(tc, fc, fc_all, w_sel, w_all, b, offs, out):
         tc.tile_pool(name="work", bufs=2) as work,
         tc.psum_pool(name="banks", bufs=2) as banks,
     ):
-        offsets = held.tile([P, LAYERS * PICKED // 16], U16, name="offsets")
-        nc.sync.dma_start(offsets[:], offs)
-
         w_sel_row = held.tile([1, LAYERS * PICKED], F32, name="w_sel_row")
         nc.scalar.dma_start(w_sel_row[:], w_sel)
-        w_all_row = held.tile([1, WHOLE], F32, name="w_all_row")
-        nc.scalar.dma_start(w_all_row[:], w_all)
         b_row = held.tile([1, 1], F32, name="b_row")
         nc.scalar.dma_start(b_row[:], b.unsqueeze(0))
 
+        offsets = held.tile([P, LAYERS * PICKED // 16], U16, name="offsets")
+        w_all_row = held.tile([1, WHOLE], F32, name="w_all_row")
         windows = {}
         for layer in range(LAYERS):
             for blk in range(BLOCKS):
                 windows[layer, blk] = held.tile([P, UNITS], F32, name=f"window{layer}{blk}")
                 nc.sync.dma_start(windows[layer, blk][:], fc[layer, blk * P : (blk + 1) * P, :])
+                if (layer, blk) == (0, 0):
+                    nc.sync.dma_start(offsets[:], offs)
+                    nc.sync.dma_start(w_all_row[:], w_all)
         kept = {}
         for blk in range(BLOCKS):
             kept[blk] = held.tile([P, WHOLE], F32, name=f"kept{blk}")

@@ -24,7 +24,7 @@ def tile_average_model_fwrf_kernel(tc, fc, fc_all, w_sel, w_all, b, offs, out):
     nc = tc.nc
     with (
         tc.tile_pool(name="held", bufs=1) as held,
-        tc.tile_pool(name="work", bufs=2) as work,
+        tc.tile_pool(name="work", bufs=BLOCKS * LAYERS) as work,
         tc.psum_pool(name="banks", bufs=2) as banks,
     ):
         w_sel_row = held.tile([1, LAYERS * PICKED], F32, name="w_sel_row")

@@ -3,7 +3,6 @@ import concourse.mybir as mybir
 F32 = mybir.dt.float32
 U16 = mybir.dt.uint16
 MULT = mybir.AluOpType.mult
-ADD = mybir.AluOpType.add
 IDENTITY = mybir.ActivationFunctionType.Identity
 
 P = 128
@@ -11,9 +10,12 @@ LAYERS = 2
 SAMPLES = 256
 UNITS = 4096
 PICKED = 1024
+PIECE = 512
 WHOLE = 1000
 BLOCKS = SAMPLES // P
 BANK = 512
+SUMS = LAYERS * PICKED // PIECE
+EXTRAS = SUMS + 1
 SQUARE = 32
 MASS = 0.3829249225480262
 
@@ -24,14 +26,14 @@ def tile_average_model_fwrf_kernel(tc, fc, fc_all, w_sel, w_all, b, offs, out):
     nc = tc.nc
     with (
         tc.tile_pool(name="held", bufs=1) as held,
-        tc.tile_pool(name="work", bufs=BLOCKS * LAYERS) as work,
+        tc.tile_pool(name="work", bufs=BLOCKS * SUMS) as work,
         tc.psum_pool(name="banks", bufs=2) as banks,
     ):
-        w_sel_row = held.tile([1, LAYERS * PICKED], F32, name="w_sel_row")
-        nc.scalar.dma_start(w_sel_row[:], w_sel)
         b_row = held.tile([1, 1], F32, name="b_row")
         nc.scalar.dma_start(b_row[:], b.unsqueeze(0))
 
+        w_sel_row = held.tile([1, LAYERS * PICKED], F32, name="w_sel_row")
+        nc.sync.dma_start(w_sel_row[:], w_sel)
         offsets = held.tile([P, LAYERS * PICKED // 16], U16, name="offsets")
         w_all_row = held.tile([1, WHOLE], F32, name="w_all_row")
         windows = {}
@@ -44,54 +46,44 @@ def tile_average_model_fwrf_kernel(tc, fc, fc_all, w_sel, w_all, b, offs, out):
                     nc.sync.dma_start(w_all_row[:], w_all)
         kept = {}
         for blk in range(BLOCKS):
-            kept[blk] = held.tile([P, WHOLE], F32, name=f"kept{blk}")
-            nc.sync.dma_start(kept[blk][:], fc_all[blk * P : (blk + 1) * P, :])
+            kept[blk] = held.tile([P, WHOLE + EXTRAS], F32, name=f"kept{blk}")
+            nc.sync.dma_start(kept[blk][:, 0:WHOLE], fc_all[blk * P : (blk + 1) * P, :])
 
         ones = held.tile([1, P], F32, name="ones")
         nc.gpsimd.memset(ones[:], 1.0)
 
         w_sel_rows = held.tile([P, LAYERS * PICKED], F32, name="w_sel_rows")
-        w_all_rows = held.tile([P, WHOLE], F32, name="w_all_rows")
-        b_rows = held.tile([P, 1], F32, name="b_rows")
-        for row, rows in ((w_sel_row, w_sel_rows), (w_all_row, w_all_rows), (b_row, b_rows)):
-            width = rows.shape[1]
+        w_all_rows = held.tile([P, WHOLE + EXTRAS], F32, name="w_all_rows")
+        nc.gpsimd.memset(w_all_rows[:, WHOLE:], 1.0)
+        for row, rows, width in ((w_sel_row, w_sel_rows, LAYERS * PICKED), (w_all_row, w_all_rows, WHOLE)):
             for start in range(0, width, BANK):
                 end = min(start + BANK, width)
                 bank = banks.tile([P, BANK], F32, name="bank")
                 nc.tensor.matmul(bank[:, : end - start], ones[:], row[:, start:end], start=True, stop=True)
-                nc.scalar.copy(rows[:, start:end], bank[:, : end - start])
+                nc.scalar.mul(rows[:, start:end], bank[:, : end - start], MASS)
 
-        sel_sums = held.tile([P, BLOCKS * LAYERS], F32, name="sel_sums")
-        sel_total = held.tile([P, BLOCKS], F32, name="sel_total")
-        all_sums = held.tile([P, BLOCKS], F32, name="all_sums")
+        b_bank = banks.tile([P, BANK], F32, name="bank")
+        nc.tensor.matmul(b_bank[:, 0:1], ones[:], b_row[:], start=True, stop=True)
+        for blk in range(BLOCKS):
+            nc.scalar.copy(kept[blk][:, WHOLE + SUMS :], b_bank[:, 0:1])
 
         for layer in range(LAYERS):
             for blk in range(BLOCKS):
-                picked = windows[layer, blk][:].indirect(
-                    offsets[:, layer * (PICKED // 16) : (layer + 1) * (PICKED // 16)]
-                )
-                prod = work.tile([P, PICKED], F32, name="prod")
-                nc.vector.tensor_tensor(prod[:], picked, w_sel_rows[:, layer * PICKED : (layer + 1) * PICKED], MULT)
-                col = blk * LAYERS + layer
-                nc.scalar.activation(prod[:], prod[:], IDENTITY, scale=MASS, accum_out=sel_sums[:, col : col + 1])
-
-        for blk in range(BLOCKS):
-            both = work.tile([P, LAYERS], F32, name="both")
-            nc.scalar.activation(
-                both[:], sel_sums[:, blk * LAYERS : (blk + 1) * LAYERS], IDENTITY,
-                accum_out=sel_total[:, blk : blk + 1],
-            )
-
-        for blk in range(BLOCKS):
-            kept_prod = work.tile([P, WHOLE], F32, name="kept_prod")
-            nc.vector.scalar_tensor_tensor(
-                kept_prod[:], kept[blk][:], MASS, w_all_rows[:], MULT, MULT,
-                accum_out=all_sums[:, blk : blk + 1],
-            )
+                for piece in range(layer * PICKED // PIECE, (layer + 1) * PICKED // PIECE):
+                    picked = windows[layer, blk][:].indirect(offsets[:, piece * PIECE // 16 : (piece + 1) * PIECE // 16])
+                    prod = work.tile([P, PIECE], F32, name="prod")
+                    nc.vector.tensor_tensor(prod[:], picked, w_sel_rows[:, piece * PIECE : (piece + 1) * PIECE], MULT)
+                    nc.scalar.activation(
+                        prod[:], prod[:], IDENTITY, accum_out=kept[blk][:, WHOLE + piece : WHOLE + piece + 1]
+                    )
 
         columns = held.tile([P, SQUARE], F32, name="columns", align_bytes=64)
         nc.gpsimd.memset(columns[:], 0.0)
-        nc.vector.scalar_tensor_tensor(columns[:, 0:BLOCKS], all_sums[:], b_rows[:], sel_total[:], ADD, ADD)
+        for blk in range(BLOCKS):
+            kept_prod = held.tile([P, WHOLE + EXTRAS], F32, name=f"kept_prod{blk}")
+            nc.vector.scalar_tensor_tensor(
+                kept_prod[:], kept[blk][:], 1.0, w_all_rows[:], MULT, MULT, accum_out=columns[:, blk : blk + 1]
+            )
 
         squares = held.tile([P, SQUARE], F32, name="squares", align_bytes=64)
         nc.vector.transpose(squares[:], columns[:])

@@ -29,11 +29,11 @@ def tile_average_model_fwrf_kernel(tc, fc, fc_all, w_sel, w_all, b, offs, out):
         tc.tile_pool(name="work", bufs=BLOCKS * SUMS) as work,
         tc.psum_pool(name="banks", bufs=2) as banks,
     ):
+        w_sel_row = held.tile([1, LAYERS * PICKED], F32, name="w_sel_row")
+        nc.scalar.dma_start(w_sel_row[:], w_sel)
         b_row = held.tile([1, 1], F32, name="b_row")
         nc.scalar.dma_start(b_row[:], b.unsqueeze(0))
 
-        w_sel_row = held.tile([1, LAYERS * PICKED], F32, name="w_sel_row")
-        nc.sync.dma_start(w_sel_row[:], w_sel)
         offsets = held.tile([P, LAYERS * PICKED // 16], U16, name="offsets")
         w_all_row = held.tile([1, WHOLE], F32, name="w_all_row")
         windows = {}

@@ -77,18 +77,19 @@ def tile_average_model_fwrf_kernel(tc, fc, fc_all, w_sel, w_all, b, offs, out):
                         prod[:], prod[:], IDENTITY, accum_out=kept[blk][:, WHOLE + piece : WHOLE + piece + 1]
                     )
 
-        columns = held.tile([P, SQUARE], F32, name="columns", align_bytes=64)
-        nc.gpsimd.memset(columns[:], 0.0)
+        columns = {}
         for blk in range(BLOCKS):
+            columns[blk] = held.tile([P, SQUARE], F32, name=f"columns{blk}", align_bytes=64)
+            nc.gpsimd.memset(columns[blk][:], 0.0)
             kept_prod = held.tile([P, WHOLE + EXTRAS], F32, name=f"kept_prod{blk}")
             nc.vector.scalar_tensor_tensor(
-                kept_prod[:], kept[blk][:], 1.0, w_all_rows[:], MULT, MULT, accum_out=columns[:, blk : blk + 1]
+                kept_prod[:], kept[blk][:], 1.0, w_all_rows[:], MULT, MULT, accum_out=columns[blk][:, 0:1]
             )
 
-        squares = held.tile([P, SQUARE], F32, name="squares", align_bytes=64)
-        nc.vector.transpose(squares[:], columns[:])
+        squares = held.tile([P, BLOCKS * SQUARE], F32, name="squares", align_bytes=64)
         for blk in range(BLOCKS):
-            nc.sync.dma_start(
-                out[blk * P : (blk + 1) * P, :].rearrange("(q i) one -> q (i one)", i=SQUARE),
-                squares[blk:P:SQUARE, :],
-            )
+            nc.vector.transpose(squares[:, blk * SQUARE : (blk + 1) * SQUARE], columns[blk][:])
+        nc.sync.dma_start(
+            out.rearrange("(b q i) one -> q b (i one)", b=BLOCKS, i=SQUARE),
+            squares[0:P:SQUARE, :].rearrange("q (b i) -> q b i", b=BLOCKS),
+        )

@@ -40,7 +40,9 @@ def tile_average_model_fwrf_kernel(tc, fc, fc_all, w_sel, w_all, b, offs, out):
         for layer in range(LAYERS):
             for blk in range(BLOCKS):
                 windows[layer, blk] = held.tile([P, UNITS], F32, name=f"window{layer}{blk}")
-                nc.sync.dma_start(windows[layer, blk][:], fc[layer, blk * P : (blk + 1) * P, :])
+                rows = fc[layer, blk * P : (blk + 1) * P, :].rearrange("(p two) u -> two p u", two=2)
+                nc.sync.dma_start(windows[layer, blk][0:P:2, :], rows[0])
+                nc.scalar.dma_start(windows[layer, blk][1:P:2, :], rows[1])
                 if (layer, blk) == (0, 0):
                     nc.sync.dma_start(offsets[:], offs)
                     nc.sync.dma_start(w_all_row[:], w_all)

@@ -27,7 +27,7 @@ def tile_average_model_fwrf_kernel(tc, fc, fc_all, w_sel, w_all, b, offs, out):
     with (
         tc.tile_pool(name="held", bufs=1) as held,
         tc.tile_pool(name="work", bufs=BLOCKS * SUMS) as work,
-        tc.psum_pool(name="banks", bufs=2) as banks,
+        tc.psum_pool(name="banks", bufs=4) as banks,
     ):
         w_sel_row = held.tile([1, LAYERS * PICKED], F32, name="w_sel_row")
         nc.scalar.dma_start(w_sel_row[:], w_sel)
@@ -49,7 +49,7 @@ def tile_average_model_fwrf_kernel(tc, fc, fc_all, w_sel, w_all, b, offs, out):
         kept = {}
         for blk in range(BLOCKS):
             kept[blk] = held.tile([P, WHOLE + EXTRAS], F32, name=f"kept{blk}")
-            nc.sync.dma_start(kept[blk][:, 0:WHOLE], fc_all[blk * P : (blk + 1) * P, :])
+            nc.scalar.dma_start(kept[blk][:, 0:WHOLE], fc_all[blk * P : (blk + 1) * P, :])
 
         ones = held.tile([1, P], F32, name="ones")
         nc.gpsimd.memset(ones[:], 1.0)

import concourse.mybir as mybir

F32 = mybir.dt.float32
U16 = mybir.dt.uint16
MULT = mybir.AluOpType.mult
IDENTITY = mybir.ActivationFunctionType.Identity

P = 128
LAYERS = 2
SAMPLES = 256
UNITS = 4096
PICKED = 1024
PIECE = 512
WHOLE = 1000
BLOCKS = SAMPLES // P
BANK = 512
SUMS = LAYERS * PICKED // PIECE
EXTRAS = SUMS + 1
SQUARE = 32
MASS = 0.3829249225480262

FLOPS = 2 * SAMPLES * (LAYERS * PICKED + WHOLE)


def tile_average_model_fwrf_kernel(tc, fc, fc_all, w_sel, w_all, b, offs, out):
    nc = tc.nc
    with (
        tc.tile_pool(name="held", bufs=1) as held,
        tc.tile_pool(name="work", bufs=BLOCKS * SUMS) as work,
        tc.psum_pool(name="banks", bufs=4) as banks,
    ):
        w_sel_row = held.tile([1, LAYERS * PICKED], F32, name="w_sel_row")
        nc.scalar.dma_start(w_sel_row[:], w_sel)
        b_row = held.tile([1, 1], F32, name="b_row")
        nc.scalar.dma_start(b_row[:], b.unsqueeze(0))

        offsets = held.tile([P, LAYERS * PICKED // 16], U16, name="offsets")
        w_all_row = held.tile([1, WHOLE], F32, name="w_all_row")
        windows = {}
        for layer in range(LAYERS):
            for blk in range(BLOCKS):
                windows[layer, blk] = held.tile([P, UNITS], F32, name=f"window{layer}{blk}")
                rows = fc[layer, blk * P : (blk + 1) * P, :].rearrange("(p two) u -> two p u", two=2)
                nc.sync.dma_start(windows[layer, blk][0:P:2, :], rows[0])
                nc.scalar.dma_start(windows[layer, blk][1:P:2, :], rows[1])
                if (layer, blk) == (0, 0):
                    nc.sync.dma_start(offsets[:], offs)
                    nc.sync.dma_start(w_all_row[:], w_all)
        kept = {}
        for blk in range(BLOCKS):
            kept[blk] = held.tile([P, WHOLE + EXTRAS], F32, name=f"kept{blk}")
            nc.scalar.dma_start(kept[blk][:, 0:WHOLE], fc_all[blk * P : (blk + 1) * P, :])

        ones = held.tile([1, P], F32, name="ones")
        nc.gpsimd.memset(ones[:], 1.0)

        w_sel_rows = held.tile([P, LAYERS * PICKED], F32, name="w_sel_rows")
        w_all_rows = held.tile([P, WHOLE + EXTRAS], F32, name="w_all_rows")
        nc.gpsimd.memset(w_all_rows[:, WHOLE:], 1.0)
        for row, rows, width in ((w_sel_row, w_sel_rows, LAYERS * PICKED), (w_all_row, w_all_rows, WHOLE)):
            for start in range(0, width, BANK):
                end = min(start + BANK, width)
                bank = banks.tile([P, BANK], F32, name="bank")
                nc.tensor.matmul(bank[:, : end - start], ones[:], row[:, start:end], start=True, stop=True)
                nc.scalar.mul(rows[:, start:end], bank[:, : end - start], MASS)

        b_bank = banks.tile([P, BANK], F32, name="bank")
        nc.tensor.matmul(b_bank[:, 0:1], ones[:], b_row[:], start=True, stop=True)
        for blk in range(BLOCKS):
            nc.scalar.copy(kept[blk][:, WHOLE + SUMS :], b_bank[:, 0:1])

        for layer in range(LAYERS):
            for blk in range(BLOCKS):
                for piece in range(layer * PICKED // PIECE, (layer + 1) * PICKED // PIECE):
                    picked = windows[layer, blk][:].indirect(offsets[:, piece * PIECE // 16 : (piece + 1) * PIECE // 16])
                    prod = work.tile([P, PIECE], F32, name="prod")
                    nc.vector.tensor_tensor(prod[:], picked, w_sel_rows[:, piece * PIECE : (piece + 1) * PIECE], MULT)
                    nc.scalar.activation(
                        prod[:], prod[:], IDENTITY, accum_out=kept[blk][:, WHOLE + piece : WHOLE + piece + 1]
                    )

        columns = {}
        for blk in range(BLOCKS):
            columns[blk] = held.tile([P, SQUARE], F32, name=f"columns{blk}", align_bytes=64)
            nc.gpsimd.memset(columns[blk][:], 0.0)
            kept_prod = held.tile([P, WHOLE + EXTRAS], F32, name=f"kept_prod{blk}")
            nc.vector.scalar_tensor_tensor(
                kept_prod[:], kept[blk][:], 1.0, w_all_rows[:], MULT, MULT, accum_out=columns[blk][:, 0:1]
            )

        squares = held.tile([P, BLOCKS * SQUARE], F32, name="squares", align_bytes=64)
        for blk in range(BLOCKS):
            nc.vector.transpose(squares[:, blk * SQUARE : (blk + 1) * SQUARE], columns[blk][:])
        nc.sync.dma_start(
            out.rearrange("(b q i) one -> q b (i one)", b=BLOCKS, i=SQUARE),
            squares[0:P:SQUARE, :].rearrange("q (b i) -> q b i", b=BLOCKS),
        )
